import numpy as np
import ml_dtypes


def mxq(x, axis, fmt="e4m3"):
    dtype, down = {"e4m3": (ml_dtypes.float8_e4m3fn, 7), "e5m2": (ml_dtypes.float8_e5m2, 14)}[fmt]
    v = np.moveaxis(np.asarray(x, np.float32).astype(ml_dtypes.bfloat16).astype(np.float64), axis, -1)
    blocks = v.reshape(v.shape[:-1] + (-1, 32))
    amax = np.abs(blocks).max(-1, keepdims=True)
    byte = np.maximum(np.where(amax > 0, np.frexp(amax)[1] - 1 + 127, 0) - down, 1)
    scale = np.exp2(byte - 127.0)
    codes = (blocks / scale).astype(np.float32).astype(dtype).astype(np.float64)
    return np.moveaxis((codes * scale).reshape(v.shape), -1, axis)


WIDE = False


def mx_kscale(k):
    if not WIDE:
        return np.ones(k)
    levels = np.array([20, -20, 10, -10, 0])
    a = np.random.permutation(np.resize(levels, k // 512 * 4)).reshape(k // 512, 4)
    idx = np.arange(k)
    return np.exp2(a[idx // 512, idx % 128 // 32])


BF16 = ml_dtypes.bfloat16


def bf(x):
    return np.asarray(x, np.float32).astype(BF16)


def f64(x):
    return np.asarray(x).astype(np.float64)


B, T, D, NH, HD, G, RD, F = 1, 512, 8192, 8, 128, 2, 16, 4096
HKV = NH // G
C = NH * HD


def setup_inputs():
    u = mx_kscale(D)
    v = np.random.standard_normal((B, HKV, T, HD))
    a = 0.4 * np.random.standard_normal((B, HKV, G, T, HD)) + 0.4 * v[:, :, None]
    x = np.random.standard_normal((B, T, D)) * np.random.uniform(0.5, 2.0, (B, T, 1))
    wo = np.random.standard_normal((D, C)) / np.sqrt(C) / u[:, None]
    sc = 1.0 + 0.1 * np.random.standard_normal(D)
    g = 4.0 * np.random.standard_normal((B, T, D)) * np.exp2(np.random.randint(-12, 1, (B, T, 1))) * u
    return {"attn_out": bf(a),
            "v": bf(v),
            "x": bf(x),
            "wo": bf(wo),
            "attn_scale": bf(sc),
            "grad_out": bf(g)}


def reference(attn_out, v, x, wo, attn_scale, grad_out):
    gs = f64(grad_out) * f64(attn_scale)
    gy = mxq(gs, 2, "e5m2") @ mxq(f64(wo), 0, "e4m3")
    gy = gy.reshape(B, T, HKV, G, HD)
    v_t = f64(v).transpose(0, 2, 1, 3)
    vn = v_t / np.maximum(np.sqrt(np.sum(np.square(v_t), axis=-1, keepdims=True)), 1e-12)
    vn = vn[:, :, :, None, :]
    ga = gy - np.sum(gy * vn, axis=-1, keepdims=True) * vn
    return ga.transpose(0, 2, 3, 1, 4)

@@ -1,0 +1,273 @@
+from contextlib import ExitStack
+
+import concourse.mybir as mybir
+from concourse.masks import make_identity
+
+BF16 = mybir.dt.bfloat16
+F32 = mybir.dt.float32
+U32 = mybir.dt.uint32
+U8 = mybir.dt.uint8
+E4M3_X4 = mybir.dt.float8_e4m3fn_x4
+E5M2_X4 = mybir.dt.float8_e5m2_x4
+ALU = mybir.AluOpType
+ACT = mybir.ActivationFunctionType
+
+P = 128
+TOKENS = 512
+D = 8192
+KV_HEADS = 4
+GROUP = 2
+HEAD_DIM = 128
+C = KV_HEADS * GROUP * HEAD_DIM
+PACK = 4
+K_PASS = P * PACK
+PASSES = D // K_PASS
+TOKEN_TILES = TOKENS // P
+CHUNK_PASSES = 4
+CHUNK = CHUNK_PASSES * K_PASS
+CHUNKS = D // CHUNK
+N_TILE = 512
+HALVES = C // N_TILE
+BANK_HEADS = N_TILE // HEAD_DIM
+EARLY_TILES = 3
+LOAD_AHEAD = 2
+
+FLOPS = 2 * TOKENS * D * C
+BYTES = 2 * (D * C + TOKENS * D + KV_HEADS * TOKENS * HEAD_DIM + D) + 4 * TOKENS * C
+
+
+def g_chunk_of_slot(slot):
+    if 0 <= slot < PASSES:
+        chunk, i = divmod(slot, CHUNK_PASSES)
+        return (i, chunk) if i < EARLY_TILES else None
+    if PASSES <= slot < PASSES + CHUNKS:
+        return (EARLY_TILES, slot - PASSES)
+    return None
+
+
+def tile_block_pb_k_kernel(tc, attn_out, v, x, wo, attn_scale, grad_out, out):
+    nc = tc.nc
+    g_view = grad_out[0].rearrange("(p j) k -> p j k", j=TOKEN_TILES)
+    v_view = v[0].rearrange("h (p j) d -> p h (j d)", j=TOKEN_TILES)
+    out_view = out[0].rearrange("h g (p j) d -> p j (h g) d", j=TOKEN_TILES)
+
+    with ExitStack() as ctx:
+        const = ctx.enter_context(tc.tile_pool(name="const", bufs=1))
+        keep = ctx.enter_context(tc.tile_pool(name="keep", bufs=1))
+        raw = ctx.enter_context(tc.tile_pool(name="raw", bufs=LOAD_AHEAD + 1))
+        stage = ctx.enter_context(tc.tile_pool(name="stage", bufs=3))
+        tail = ctx.enter_context(tc.tile_pool(name="tail", bufs=3))
+        acc_pool = ctx.enter_context(tc.psum_pool(name="acc", bufs=1))
+        tp_pool = ctx.enter_context(tc.psum_pool(name="tp", bufs=2))
+
+        ident = const.tile([P, P], F32)
+        make_identity(nc, ident[:])
+
+        v_sb = const.tile([P, KV_HEADS, TOKEN_TILES, HEAD_DIM], BF16)
+        nc.scalar.dma_start(out=v_sb[:].rearrange("p h j d -> p h (j d)"), in_=v_view)
+
+        sc_rows = const.tile([P, 2 * P], BF16)
+        nc.vector.memset(sc_rows[:], 0.0)
+        nc.sync.dma_start(
+            out=sc_rows[0 : D // (2 * P), :], in_=attn_scale.rearrange("(r w) -> r w", w=2 * P)
+        )
+        sc_ps = tp_pool.tile([P, PACK, P], F32, tag="tp")
+        nc.tensor.transpose(sc_ps[:, 0, :], sc_rows[:].bitcast(F32), ident[:])
+        sc_t = const.tile([P, PASSES * PACK], BF16)
+        nc.vector.tensor_copy(out=sc_t[:].bitcast(F32), in_=sc_ps[:, 0, 0 : PASSES * 2])
+        sc_view = sc_t[:].rearrange("p (c t) -> p c t", t=PACK)
+
+        gs_codes = keep.tile([P, TOKEN_TILES * PASSES * P], U32, align_bytes=64)
+        gs_scales = keep.tile([P, TOKEN_TILES * PASSES * P], U8, align_bytes=64)
+        w_codes = keep.tile([P, PASSES * C], U32, align_bytes=64)
+        w_scales = keep.tile([P, PASSES * C], U8, align_bytes=64)
+
+        sq = const.tile([P, KV_HEADS, TOKEN_TILES, HEAD_DIM], BF16)
+        ss = const.tile([P, KV_HEADS * TOKEN_TILES], F32)
+
+        acc = {}
+        for j in range(EARLY_TILES):
+            for n in range(HALVES):
+                acc[(j, n)] = acc_pool.tile([P, N_TILE], F32, name="acc%d%d" % (j, n))
+
+        def load_g(j, chunk):
+            g_raw = raw.tile([P, CHUNK], BF16, tag="g_raw")
+            nc.sync.dma_start(out=g_raw[:], in_=g_view[:, j, chunk * CHUNK : (chunk + 1) * CHUNK])
+            return g_raw
+
+        def load_w(c):
+            w_raw = raw.tile([P, PACK, C], BF16, tag="w_raw")
+            nc.sync.dma_start(
+                out=w_raw[:].rearrange("p (u e) n -> p u (e n)", u=2),
+                in_=wo[c * K_PASS : (c + 1) * K_PASS, :].rearrange(
+                    "(u q e) n -> q u (e n)", u=2, e=2
+                ),
+            )
+            return w_raw
+
+        def transpose_g(g_raw):
+            g_t = stage.tile([P, CHUNK], BF16, tag="g_t")
+            words = g_raw[:].bitcast(F32)
+            g_t_words = g_t[:].bitcast(F32).rearrange("p (c r u) -> p c r u", c=CHUNK_PASSES, u=2)
+            for b in range(2):
+                xt = tp_pool.tile([P, PACK, P], F32, tag="tp")
+                for s in range(PACK):
+                    w0 = (PACK * b + s) * P
+                    nc.tensor.transpose(xt[:, s, :], words[:, w0 : w0 + P], ident[:])
+                nc.scalar.copy(
+                    out=g_t_words[:, 2 * b : 2 * b + 2, :, :],
+                    in_=xt[:].rearrange("p (c u) r -> p c r u", u=2),
+                )
+            return g_t
+
+        def scale_g(g_t, chunk):
+            gs_t = stage.tile([P, CHUNK], BF16, tag="gs_t", align_bytes=64)
+            nc.vector.tensor_tensor(
+                out=gs_t[:].rearrange("p (c r t) -> p c r t", c=CHUNK_PASSES, t=PACK),
+                in0=g_t[:].rearrange("p (c r t) -> p c r t", c=CHUNK_PASSES, t=PACK),
+                in1=sc_view[:, chunk * CHUNK_PASSES : (chunk + 1) * CHUNK_PASSES, :]
+                .unsqueeze(2)
+                .to_broadcast([P, CHUNK_PASSES, P, PACK]),
+                op=ALU.mult,
+            )
+            return gs_t
+
+        def quantise_g(gs_t, j, chunk):
+            col = (j * PASSES + chunk * CHUNK_PASSES) * P
+            cols = slice(col, col + CHUNK_PASSES * P)
+            nc.vector.quantize_mx(
+                out=gs_codes[:, cols].bitcast(E5M2_X4), scales=gs_scales[:, cols], in_=gs_t[:]
+            )
+
+        def regroup_w(w_raw):
+            halves = []
+            for n, copy in enumerate((nc.scalar.copy, nc.vector.tensor_copy)):
+                w_grp = stage.tile([P, N_TILE, PACK], BF16, tag="w_grp%d" % n, align_bytes=64)
+                copy(
+                    out=w_grp[:].rearrange("p (c i) t -> p c t i", i=4),
+                    in_=w_raw[:, :, n * N_TILE : (n + 1) * N_TILE].rearrange(
+                        "p t (c i) -> p c t i", i=4
+                    ),
+                )
+                halves.append(w_grp)
+            return halves
+
+        def quantise_w(halves, c):
+            for n in range(HALVES):
+                cols = slice(c * C + n * N_TILE, c * C + (n + 1) * N_TILE)
+                nc.vector.quantize_mx(
+                    out=w_codes[:, cols].bitcast(E4M3_X4),
+                    scales=w_scales[:, cols],
+                    in_=halves[n][:].rearrange("p n t -> p (n t)"),
+                )
+
+        def multiply(j, c):
+            g_cols = slice((j * PASSES + c) * P, (j * PASSES + c + 1) * P)
+            for n in range(HALVES):
+                w_cols = slice(c * C + n * N_TILE, c * C + (n + 1) * N_TILE)
+                nc.tensor.matmul_mx(
+                    out=acc[(j, n)][:],
+                    lhsT=gs_codes[:, g_cols].bitcast(E5M2_X4),
+                    lhsT_scale=gs_scales[:, g_cols],
+                    rhs=w_codes[:, w_cols].bitcast(E4M3_X4),
+                    rhs_scale=w_scales[:, w_cols],
+                    start=(c == 0),
+                    stop=(c == PASSES - 1),
+                )
+
+        def square_v(h):
+            for j in range(TOKEN_TILES):
+                nc.scalar.activation(
+                    out=sq[:, h, j, :],
+                    in_=v_sb[:, h, j, :],
+                    func=ACT.Square,
+                    accum_out=ss[:, h * TOKEN_TILES + j : h * TOKEN_TILES + j + 1],
+                )
+
+        g_raw_of, g_t_of, w_raw_of, w_grp_of = {}, {}, {}, {}
+        for slot in range(-LOAD_AHEAD, PASSES + CHUNKS):
+            ahead = slot + LOAD_AHEAD
+            if g_chunk_of_slot(ahead) is not None:
+                g_raw_of[ahead] = load_g(*g_chunk_of_slot(ahead))
+            if 0 <= ahead < PASSES:
+                w_raw_of[ahead] = load_w(ahead)
+            if g_chunk_of_slot(slot + 1) is not None:
+                g_t_of[slot + 1] = transpose_g(g_raw_of[slot + 1])
+            mine = g_chunk_of_slot(slot)
+            if mine is not None:
+                gs_t = scale_g(g_t_of[slot], mine[1])
+            if 0 <= slot < PASSES:
+                w_grp_of[slot] = regroup_w(w_raw_of[slot])
+                if mine is None:
+                    square_v(slot // CHUNK_PASSES)
+            if mine is not None:
+                quantise_g(gs_t, mine[0], mine[1])
+            if 0 <= slot - 1 < PASSES:
+                quantise_w(w_grp_of[slot - 1], slot - 1)
+            if 0 <= slot - 2 < PASSES:
+                for j in range(EARLY_TILES):
+                    multiply(j, slot - 2)
+
+        for n in range(HALVES):
+            acc[(EARLY_TILES, n)] = tp_pool.tile([P, N_TILE], F32, tag="tp", name="acc_late%d" % n)
+        for c in range(PASSES):
+            multiply(EARLY_TILES, c)
+
+        neg_ss = const.tile([P, KV_HEADS, TOKEN_TILES], F32)
+        neg_inv = const.tile([P, KV_HEADS, TOKEN_TILES], F32)
+        nc.vector.tensor_scalar(
+            out=neg_ss[:].rearrange("p h j -> p (h j)"),
+            in0=ss[:],
+            scalar1=1e-24,
+            scalar2=-1.0,
+            op0=ALU.max,
+            op1=ALU.mult,
+        )
+        nc.vector.reciprocal(out=neg_inv[:], in_=neg_ss[:])
+
+        def start_projection(j, n):
+            prod = tail.tile([P, BANK_HEADS, HEAD_DIM], F32, tag="prod")
+            nc.vector.tensor_tensor(
+                out=prod[:].rearrange("p (h g) d -> p h g d", g=GROUP),
+                in0=acc[(j, n)][:].rearrange("p (h g d) -> p h g d", g=GROUP, d=HEAD_DIM),
+                in1=v_sb[:, 2 * n : 2 * n + 2, j, :]
+                .unsqueeze(2)
+                .to_broadcast([P, 2, GROUP, HEAD_DIM]),
+                op=ALU.mult,
+            )
+            dot = tail.tile([P, BANK_HEADS], F32, tag="dot")
+            for q in range(BANK_HEADS):
+                nc.scalar.activation(
+                    out=prod[:, q, :], in_=prod[:, q, :], func=ACT.Copy, accum_out=dot[:, q : q + 1]
+                )
+            return dot
+
+        def finish_projection(j, n, dot):
+            coef = tail.tile([P, BANK_HEADS], F32, tag="coef")
+            nc.vector.tensor_tensor(
+                out=coef[:].rearrange("p (h g) -> p h g", g=GROUP),
+                in0=dot[:].rearrange("p (h g) -> p h g", g=GROUP),
+                in1=neg_inv[:, 2 * n : 2 * n + 2, j : j + 1].to_broadcast([P, 2, GROUP]),
+                op=ALU.mult,
+            )
+            res = tail.tile([P, BANK_HEADS, HEAD_DIM], F32, tag="res")
+            for q in range(BANK_HEADS):
+                nc.vector.scalar_tensor_tensor(
+                    out=res[:, q, :],
+                    in0=v_sb[:, 2 * n + q // GROUP, j, :],
+                    scalar=coef[:, q : q + 1],
+                    in1=acc[(j, n)][:, q * HEAD_DIM : (q + 1) * HEAD_DIM],
+                    op0=ALU.mult,
+                    op1=ALU.add,
+                )
+            nc.sync.dma_start(
+                out=out_view[:, j, n * BANK_HEADS : (n + 1) * BANK_HEADS, :], in_=res[:]
+            )
+
+        banks = [(j, n) for j in range(TOKEN_TILES) for n in range(HALVES)]
+        dots = {}
+        for b, bank in enumerate(banks):
+            dots[bank] = start_projection(*bank)
+            if b > 0:
+                finish_projection(*banks[b - 1], dots[banks[b - 1]])
+        finish_projection(*banks[-1], dots[banks[-1]])

@@ -59,6 +59,7 @@ def tile_block_pb_k_kernel(tc, attn_out, v, x, wo, attn_scale, grad_out, out):
         tail = ctx.enter_context(tc.tile_pool(name="tail", bufs=3))
         acc_pool = ctx.enter_context(tc.psum_pool(name="acc", bufs=1))
         tp_pool = ctx.enter_context(tc.psum_pool(name="tp", bufs=2))
+        ctx.enter_context(tc.manual_schedule())
 
         ident = const.tile([P, P], F32)
         make_identity(nc, ident[:])

@@ -31,6 +31,7 @@ HALVES = C // N_TILE
 BANK_HEADS = N_TILE // HEAD_DIM
 EARLY_TILES = 3
 LOAD_AHEAD = 2
+SCALAR_COLS = 768
 
 FLOPS = 2 * TOKENS * D * C
 BYTES = 2 * (D * C + TOKENS * D + KV_HEADS * TOKENS * HEAD_DIM + D) + 4 * TOKENS * C
@@ -59,7 +60,6 @@ def tile_block_pb_k_kernel(tc, attn_out, v, x, wo, attn_scale, grad_out, out):
         tail = ctx.enter_context(tc.tile_pool(name="tail", bufs=3))
         acc_pool = ctx.enter_context(tc.psum_pool(name="acc", bufs=1))
         tp_pool = ctx.enter_context(tc.psum_pool(name="tp", bufs=2))
-        ctx.enter_context(tc.manual_schedule())
 
         ident = const.tile([P, P], F32)
         make_identity(nc, ident[:])
@@ -76,7 +76,6 @@ def tile_block_pb_k_kernel(tc, attn_out, v, x, wo, attn_scale, grad_out, out):
         nc.tensor.transpose(sc_ps[:, 0, :], sc_rows[:].bitcast(F32), ident[:])
         sc_t = const.tile([P, PASSES * PACK], BF16)
         nc.vector.tensor_copy(out=sc_t[:].bitcast(F32), in_=sc_ps[:, 0, 0 : PASSES * 2])
-        sc_view = sc_t[:].rearrange("p (c t) -> p c t", t=PACK)
 
         gs_codes = keep.tile([P, TOKEN_TILES * PASSES * P], U32, align_bytes=64)
         gs_scales = keep.tile([P, TOKEN_TILES * PASSES * P], U8, align_bytes=64)
@@ -106,31 +105,30 @@ def tile_block_pb_k_kernel(tc, attn_out, v, x, wo, attn_scale, grad_out, out):
             )
             return w_raw
 
-        def transpose_g(g_raw):
-            g_t = stage.tile([P, CHUNK], BF16, tag="g_t")
+        def transpose_and_scale_g(g_raw, chunk):
             words = g_raw[:].bitcast(F32)
-            g_t_words = g_t[:].bitcast(F32).rearrange("p (c r u) -> p c r u", c=CHUNK_PASSES, u=2)
+            gs_t = stage.tile([P, CHUNK], BF16, tag="gs_t", align_bytes=64)
             for b in range(2):
                 xt = tp_pool.tile([P, PACK, P], F32, tag="tp")
-                for s in range(PACK):
-                    w0 = (PACK * b + s) * P
-                    nc.tensor.transpose(xt[:, s, :], words[:, w0 : w0 + P], ident[:])
-                nc.scalar.copy(
-                    out=g_t_words[:, 2 * b : 2 * b + 2, :, :],
-                    in_=xt[:].rearrange("p (c u) r -> p c r u", u=2),
+                for c in range(2):
+                    for u in range(2):
+                        w0 = ((2 * b + c) * 2 + u) * P
+                        nc.tensor.transpose(xt[:, 2 * u + c, :], words[:, w0 : w0 + P], ident[:])
+                first = (chunk * CHUNK_PASSES + 2 * b) * PACK
+                nc.vector.tensor_tensor(
+                    out=gs_t[:, b * 2 * K_PASS : (b + 1) * 2 * K_PASS].rearrange(
+                        "p (c r u e) -> p c r u e", c=2, u=2, e=2
+                    ),
+                    in0=xt[:]
+                    .rearrange("p s r -> p (s r)")
+                    .bitcast(BF16)
+                    .rearrange("p (u c r e) -> p c r u e", u=2, c=2, e=2),
+                    in1=sc_t[:, first : first + 2 * PACK]
+                    .rearrange("p (c u e) -> p c u e", c=2, u=2)
+                    .unsqueeze(2)
+                    .to_broadcast([P, 2, P, 2, 2]),
+                    op=ALU.mult,
                 )
-            return g_t
-
-        def scale_g(g_t, chunk):
-            gs_t = stage.tile([P, CHUNK], BF16, tag="gs_t", align_bytes=64)
-            nc.vector.tensor_tensor(
-                out=gs_t[:].rearrange("p (c r t) -> p c r t", c=CHUNK_PASSES, t=PACK),
-                in0=g_t[:].rearrange("p (c r t) -> p c r t", c=CHUNK_PASSES, t=PACK),
-                in1=sc_view[:, chunk * CHUNK_PASSES : (chunk + 1) * CHUNK_PASSES, :]
-                .unsqueeze(2)
-                .to_broadcast([P, CHUNK_PASSES, P, PACK]),
-                op=ALU.mult,
-            )
             return gs_t
 
         def quantise_g(gs_t, j, chunk):
@@ -141,25 +139,24 @@ def tile_block_pb_k_kernel(tc, attn_out, v, x, wo, attn_scale, grad_out, out):
             )
 
         def regroup_w(w_raw):
-            halves = []
-            for n, copy in enumerate((nc.scalar.copy, nc.vector.tensor_copy)):
-                w_grp = stage.tile([P, N_TILE, PACK], BF16, tag="w_grp%d" % n, align_bytes=64)
+            w_grp = stage.tile([P, C, PACK], BF16, tag="w_grp", align_bytes=64)
+            for copy, cols in (
+                (nc.scalar.copy, slice(0, SCALAR_COLS)),
+                (nc.vector.tensor_copy, slice(SCALAR_COLS, C)),
+            ):
                 copy(
-                    out=w_grp[:].rearrange("p (c i) t -> p c t i", i=4),
-                    in_=w_raw[:, :, n * N_TILE : (n + 1) * N_TILE].rearrange(
-                        "p t (c i) -> p c t i", i=4
-                    ),
+                    out=w_grp[:, cols, :].rearrange("p (c i) t -> p c t i", i=4),
+                    in_=w_raw[:, :, cols].rearrange("p t (c i) -> p c t i", i=4),
                 )
-                halves.append(w_grp)
-            return halves
+            return w_grp
 
-        def quantise_w(halves, c):
+        def quantise_w(w_grp, c):
             for n in range(HALVES):
                 cols = slice(c * C + n * N_TILE, c * C + (n + 1) * N_TILE)
                 nc.vector.quantize_mx(
                     out=w_codes[:, cols].bitcast(E4M3_X4),
                     scales=w_scales[:, cols],
-                    in_=halves[n][:].rearrange("p n t -> p (n t)"),
+                    in_=w_grp[:, n * N_TILE : (n + 1) * N_TILE, :].rearrange("p n t -> p (n t)"),
                 )
 
         def multiply(j, c):
@@ -185,18 +182,16 @@ def tile_block_pb_k_kernel(tc, attn_out, v, x, wo, attn_scale, grad_out, out):
                     accum_out=ss[:, h * TOKEN_TILES + j : h * TOKEN_TILES + j + 1],
                 )
 
-        g_raw_of, g_t_of, w_raw_of, w_grp_of = {}, {}, {}, {}
+        g_raw_of, w_raw_of, w_grp_of = {}, {}, {}
         for slot in range(-LOAD_AHEAD, PASSES + CHUNKS):
             ahead = slot + LOAD_AHEAD
             if g_chunk_of_slot(ahead) is not None:
                 g_raw_of[ahead] = load_g(*g_chunk_of_slot(ahead))
             if 0 <= ahead < PASSES:
                 w_raw_of[ahead] = load_w(ahead)
-            if g_chunk_of_slot(slot + 1) is not None:
-                g_t_of[slot + 1] = transpose_g(g_raw_of[slot + 1])
             mine = g_chunk_of_slot(slot)
             if mine is not None:
-                gs_t = scale_g(g_t_of[slot], mine[1])
+                gs_t = transpose_and_scale_g(g_raw_of[slot], mine[1])
             if 0 <= slot < PASSES:
                 w_grp_of[slot] = regroup_w(w_raw_of[slot])
                 if mine is None:

@@ -25,25 +25,16 @@ PASSES = D // K_PASS
 TOKEN_TILES = TOKENS // P
 CHUNK_PASSES = 4
 CHUNK = CHUNK_PASSES * K_PASS
-CHUNKS = D // CHUNK
 N_TILE = 512
 HALVES = C // N_TILE
 BANK_HEADS = N_TILE // HEAD_DIM
 EARLY_TILES = 3
-LOAD_AHEAD = 2
+LOAD_AHEAD = 3
+MX_LAG = 3
 SCALAR_COLS = 768
 
 FLOPS = 2 * TOKENS * D * C
 BYTES = 2 * (D * C + TOKENS * D + KV_HEADS * TOKENS * HEAD_DIM + D) + 4 * TOKENS * C
-
-
-def g_chunk_of_slot(slot):
-    if 0 <= slot < PASSES:
-        chunk, i = divmod(slot, CHUNK_PASSES)
-        return (i, chunk) if i < EARLY_TILES else None
-    if PASSES <= slot < PASSES + CHUNKS:
-        return (EARLY_TILES, slot - PASSES)
-    return None
 
 
 def tile_block_pb_k_kernel(tc, attn_out, v, x, wo, attn_scale, grad_out, out):
@@ -60,6 +51,7 @@ def tile_block_pb_k_kernel(tc, attn_out, v, x, wo, attn_scale, grad_out, out):
         tail = ctx.enter_context(tc.tile_pool(name="tail", bufs=3))
         acc_pool = ctx.enter_context(tc.psum_pool(name="acc", bufs=1))
         tp_pool = ctx.enter_context(tc.psum_pool(name="tp", bufs=2))
+        ctx.enter_context(tc.manual_schedule())
 
         ident = const.tile([P, P], F32)
         make_identity(nc, ident[:])
@@ -105,37 +97,36 @@ def tile_block_pb_k_kernel(tc, attn_out, v, x, wo, attn_scale, grad_out, out):
             )
             return w_raw
 
-        def transpose_and_scale_g(g_raw, chunk):
+        def transpose_and_scale_g(g_raw, gs_t, chunk, b):
             words = g_raw[:].bitcast(F32)
-            gs_t = stage.tile([P, CHUNK], BF16, tag="gs_t", align_bytes=64)
-            for b in range(2):
-                xt = tp_pool.tile([P, PACK, P], F32, tag="tp")
-                for c in range(2):
-                    for u in range(2):
-                        w0 = ((2 * b + c) * 2 + u) * P
-                        nc.tensor.transpose(xt[:, 2 * u + c, :], words[:, w0 : w0 + P], ident[:])
-                first = (chunk * CHUNK_PASSES + 2 * b) * PACK
-                nc.vector.tensor_tensor(
-                    out=gs_t[:, b * 2 * K_PASS : (b + 1) * 2 * K_PASS].rearrange(
-                        "p (c r u e) -> p c r u e", c=2, u=2, e=2
-                    ),
-                    in0=xt[:]
-                    .rearrange("p s r -> p (s r)")
-                    .bitcast(BF16)
-                    .rearrange("p (u c r e) -> p c r u e", u=2, c=2, e=2),
-                    in1=sc_t[:, first : first + 2 * PACK]
-                    .rearrange("p (c u e) -> p c u e", c=2, u=2)
-                    .unsqueeze(2)
-                    .to_broadcast([P, 2, P, 2, 2]),
-                    op=ALU.mult,
-                )
-            return gs_t
+            xt = tp_pool.tile([P, PACK, P], F32, tag="tp")
+            for c in range(2):
+                for u in range(2):
+                    w0 = ((2 * b + c) * 2 + u) * P
+                    nc.tensor.transpose(xt[:, 2 * u + c, :], words[:, w0 : w0 + P], ident[:])
+            first = (chunk * CHUNK_PASSES + 2 * b) * PACK
+            nc.vector.tensor_tensor(
+                out=gs_t[:, b * 2 * K_PASS : (b + 1) * 2 * K_PASS].rearrange(
+                    "p (c r u e) -> p c r u e", c=2, u=2, e=2
+                ),
+                in0=xt[:]
+                .rearrange("p s r -> p (s r)")
+                .bitcast(BF16)
+                .rearrange("p (u c r e) -> p c r u e", u=2, c=2, e=2),
+                in1=sc_t[:, first : first + 2 * PACK]
+                .rearrange("p (c u e) -> p c u e", c=2, u=2)
+                .unsqueeze(2)
+                .to_broadcast([P, 2, P, 2, 2]),
+                op=ALU.mult,
+            )
 
-        def quantise_g(gs_t, j, chunk):
-            col = (j * PASSES + chunk * CHUNK_PASSES) * P
-            cols = slice(col, col + CHUNK_PASSES * P)
+        def quantise_g(gs_t, j, chunk, b):
+            col = (j * PASSES + chunk * CHUNK_PASSES + 2 * b) * P
+            cols = slice(col, col + 2 * P)
             nc.vector.quantize_mx(
-                out=gs_codes[:, cols].bitcast(E5M2_X4), scales=gs_scales[:, cols], in_=gs_t[:]
+                out=gs_codes[:, cols].bitcast(E5M2_X4),
+                scales=gs_scales[:, cols],
+                in_=gs_t[:, b * 2 * K_PASS : (b + 1) * 2 * K_PASS],
             )
 
         def regroup_w(w_raw):
@@ -159,19 +150,18 @@ def tile_block_pb_k_kernel(tc, attn_out, v, x, wo, attn_scale, grad_out, out):
                     in_=w_grp[:, n * N_TILE : (n + 1) * N_TILE, :].rearrange("p n t -> p (n t)"),
                 )
 
-        def multiply(j, c):
+        def multiply(j, c, n):
             g_cols = slice((j * PASSES + c) * P, (j * PASSES + c + 1) * P)
-            for n in range(HALVES):
-                w_cols = slice(c * C + n * N_TILE, c * C + (n + 1) * N_TILE)
-                nc.tensor.matmul_mx(
-                    out=acc[(j, n)][:],
-                    lhsT=gs_codes[:, g_cols].bitcast(E5M2_X4),
-                    lhsT_scale=gs_scales[:, g_cols],
-                    rhs=w_codes[:, w_cols].bitcast(E4M3_X4),
-                    rhs_scale=w_scales[:, w_cols],
-                    start=(c == 0),
-                    stop=(c == PASSES - 1),
-                )
+            w_cols = slice(c * C + n * N_TILE, c * C + (n + 1) * N_TILE)
+            nc.tensor.matmul_mx(
+                out=acc[(j, n)][:],
+                lhsT=gs_codes[:, g_cols].bitcast(E5M2_X4),
+                lhsT_scale=gs_scales[:, g_cols],
+                rhs=w_codes[:, w_cols].bitcast(E4M3_X4),
+                rhs_scale=w_scales[:, w_cols],
+                start=(c == 0),
+                stop=(c == PASSES - 1),
+            )
 
         def square_v(h):
             for j in range(TOKEN_TILES):
@@ -182,32 +172,41 @@ def tile_block_pb_k_kernel(tc, attn_out, v, x, wo, attn_scale, grad_out, out):
                     accum_out=ss[:, h * TOKEN_TILES + j : h * TOKEN_TILES + j + 1],
                 )
 
+        for h in range(KV_HEADS):
+            square_v(h)
+
         g_raw_of, w_raw_of, w_grp_of = {}, {}, {}
-        for slot in range(-LOAD_AHEAD, PASSES + CHUNKS):
+        for slot in range(-LOAD_AHEAD, PASSES + MX_LAG):
             ahead = slot + LOAD_AHEAD
-            if g_chunk_of_slot(ahead) is not None:
-                g_raw_of[ahead] = load_g(*g_chunk_of_slot(ahead))
-            if 0 <= ahead < PASSES:
+            preparing = 0 <= slot < PASSES
+            multiplying = 0 <= slot - MX_LAG < PASSES
+            j, chunk = slot % TOKEN_TILES, slot // TOKEN_TILES
+            if ahead < PASSES:
+                g_raw_of[ahead] = load_g(ahead % TOKEN_TILES, ahead // TOKEN_TILES)
                 w_raw_of[ahead] = load_w(ahead)
-            mine = g_chunk_of_slot(slot)
-            if mine is not None:
-                gs_t = transpose_and_scale_g(g_raw_of[slot], mine[1])
-            if 0 <= slot < PASSES:
+            if preparing:
+                gs_t = stage.tile([P, CHUNK], BF16, tag="gs_t", align_bytes=64)
+                transpose_and_scale_g(g_raw_of[slot], gs_t, chunk, 0)
                 w_grp_of[slot] = regroup_w(w_raw_of[slot])
-                if mine is None:
-                    square_v(slot // CHUNK_PASSES)
-            if mine is not None:
-                quantise_g(gs_t, mine[0], mine[1])
+                quantise_g(gs_t, j, chunk, 0)
+            if multiplying:
+                for early in range(EARLY_TILES):
+                    multiply(early, slot - MX_LAG, 0)
+            if preparing:
+                transpose_and_scale_g(g_raw_of[slot], gs_t, chunk, 1)
             if 0 <= slot - 1 < PASSES:
                 quantise_w(w_grp_of[slot - 1], slot - 1)
-            if 0 <= slot - 2 < PASSES:
-                for j in range(EARLY_TILES):
-                    multiply(j, slot - 2)
+            if preparing:
+                quantise_g(gs_t, j, chunk, 1)
+            if multiplying:
+                for early in range(EARLY_TILES):
+                    multiply(early, slot - MX_LAG, 1)
 
         for n in range(HALVES):
             acc[(EARLY_TILES, n)] = tp_pool.tile([P, N_TILE], F32, tag="tp", name="acc_late%d" % n)
         for c in range(PASSES):
-            multiply(EARLY_TILES, c)
+            for n in range(HALVES):
+                multiply(EARLY_TILES, c, n)
 
         neg_ss = const.tile([P, KV_HEADS, TOKEN_TILES], F32)
         neg_inv = const.tile([P, KV_HEADS, TOKEN_TILES], F32)

@@ -132,7 +132,8 @@ def tile_block_pb_k_kernel(tc, attn_out, v, x, wo, attn_scale, grad_out, out):
         def regroup_w(w_raw):
             w_grp = stage.tile([P, C, PACK], BF16, tag="w_grp", align_bytes=64)
             for copy, cols in (
-                (nc.scalar.copy, slice(0, SCALAR_COLS)),
+                (nc.scalar.copy, slice(0, N_TILE)),
+                (nc.scalar.copy, slice(N_TILE, SCALAR_COLS)),
                 (nc.vector.tensor_copy, slice(SCALAR_COLS, C)),
             ):
                 copy(
@@ -204,8 +205,8 @@ def tile_block_pb_k_kernel(tc, attn_out, v, x, wo, attn_scale, grad_out, out):
 
         for n in range(HALVES):
             acc[(EARLY_TILES, n)] = tp_pool.tile([P, N_TILE], F32, tag="tp", name="acc_late%d" % n)
-        for c in range(PASSES):
-            for n in range(HALVES):
+        for n in range(HALVES):
+            for c in range(PASSES):
                 multiply(EARLY_TILES, c, n)
 
         neg_ss = const.tile([P, KV_HEADS, TOKEN_TILES], F32)

@@ -231,21 +231,18 @@ def tile_block_pb_k_kernel(tc, attn_out, v, x, wo, attn_scale, grad_out, out):
                 .to_broadcast([P, 2, GROUP, HEAD_DIM]),
                 op=ALU.mult,
             )
-            dot = tail.tile([P, BANK_HEADS], F32, tag="dot")
+            coef = tail.tile([P, BANK_HEADS], F32, tag="coef")
             for q in range(BANK_HEADS):
                 nc.scalar.activation(
-                    out=prod[:, q, :], in_=prod[:, q, :], func=ACT.Copy, accum_out=dot[:, q : q + 1]
+                    out=prod[:, q, :],
+                    in_=prod[:, q, :],
+                    func=ACT.Copy,
+                    scale=neg_inv[:, 2 * n + q // GROUP, j : j + 1],
+                    accum_out=coef[:, q : q + 1],
                 )
-            return dot
+            return coef
 
-        def finish_projection(j, n, dot):
-            coef = tail.tile([P, BANK_HEADS], F32, tag="coef")
-            nc.vector.tensor_tensor(
-                out=coef[:].rearrange("p (h g) -> p h g", g=GROUP),
-                in0=dot[:].rearrange("p (h g) -> p h g", g=GROUP),
-                in1=neg_inv[:, 2 * n : 2 * n + 2, j : j + 1].to_broadcast([P, 2, GROUP]),
-                op=ALU.mult,
-            )
+        def finish_projection(j, n, coef):
             res = tail.tile([P, BANK_HEADS, HEAD_DIM], F32, tag="res")
             for q in range(BANK_HEADS):
                 nc.vector.scalar_tensor_tensor(
@@ -261,9 +258,9 @@ def tile_block_pb_k_kernel(tc, attn_out, v, x, wo, attn_scale, grad_out, out):
             )
 
         banks = [(j, n) for j in range(TOKEN_TILES) for n in range(HALVES)]
-        dots = {}
+        coefs = {}
         for b, bank in enumerate(banks):
-            dots[bank] = start_projection(*bank)
+            coefs[bank] = start_projection(*bank)
             if b > 0:
-                finish_projection(*banks[b - 1], dots[banks[b - 1]])
-        finish_projection(*banks[-1], dots[banks[-1]])
+                finish_projection(*banks[b - 1], coefs[banks[b - 1]])
+        finish_projection(*banks[-1], coefs[banks[-1]])

@@ -31,6 +31,7 @@ BANK_HEADS = N_TILE // HEAD_DIM
 EARLY_TILES = 3
 LOAD_AHEAD = 3
 MX_LAG = 3
+V_SLOT = 8
 SCALAR_COLS = 768
 
 FLOPS = 2 * TOKENS * D * C
@@ -46,6 +47,7 @@ def tile_block_pb_k_kernel(tc, attn_out, v, x, wo, attn_scale, grad_out, out):
     with ExitStack() as ctx:
         const = ctx.enter_context(tc.tile_pool(name="const", bufs=1))
         keep = ctx.enter_context(tc.tile_pool(name="keep", bufs=1))
+        first = ctx.enter_context(tc.tile_pool(name="first", bufs=1))
         raw = ctx.enter_context(tc.tile_pool(name="raw", bufs=LOAD_AHEAD + 1))
         stage = ctx.enter_context(tc.tile_pool(name="stage", bufs=3))
         tail = ctx.enter_context(tc.tile_pool(name="tail", bufs=3))
@@ -57,13 +59,15 @@ def tile_block_pb_k_kernel(tc, attn_out, v, x, wo, attn_scale, grad_out, out):
         make_identity(nc, ident[:])
 
         v_sb = const.tile([P, KV_HEADS, TOKEN_TILES, HEAD_DIM], BF16)
-        nc.scalar.dma_start(out=v_sb[:].rearrange("p h j d -> p h (j d)"), in_=v_view)
 
         sc_rows = const.tile([P, 2 * P], BF16)
         nc.vector.memset(sc_rows[:], 0.0)
         nc.sync.dma_start(
             out=sc_rows[0 : D // (2 * P), :], in_=attn_scale.rearrange("(r w) -> r w", w=2 * P)
         )
+        table = const.tile([P, 2], F32)
+        nc.vector.memset(table[:, 0:1], 0.0)
+        nc.scalar.copy(out=table[:, 1:2], in_=table[:, 0:1])
         sc_ps = tp_pool.tile([P, PACK, P], F32, tag="tp")
         nc.tensor.transpose(sc_ps[:, 0, :], sc_rows[:].bitcast(F32), ident[:])
         sc_t = const.tile([P, PASSES * PACK], BF16)
@@ -78,13 +82,18 @@ def tile_block_pb_k_kernel(tc, attn_out, v, x, wo, attn_scale, grad_out, out):
         ss = const.tile([P, KV_HEADS * TOKEN_TILES], F32)
 
         acc = {}
-        for j in range(EARLY_TILES):
-            for n in range(HALVES):
+        for n in range(HALVES):
+            for j in range(EARLY_TILES):
                 acc[(j, n)] = acc_pool.tile([P, N_TILE], F32, name="acc%d%d" % (j, n))
 
-        def load_g(j, chunk):
+        def load_g(j, chunk, pieces=1):
             g_raw = raw.tile([P, CHUNK], BF16, tag="g_raw")
-            nc.sync.dma_start(out=g_raw[:], in_=g_view[:, j, chunk * CHUNK : (chunk + 1) * CHUNK])
+            width = CHUNK // pieces
+            for i in range(pieces):
+                k0 = chunk * CHUNK + i * width
+                nc.sync.dma_start(
+                    out=g_raw[:, i * width : (i + 1) * width], in_=g_view[:, j, k0 : k0 + width]
+                )
             return g_raw
 
         def load_w(c):
@@ -96,6 +105,17 @@ def tile_block_pb_k_kernel(tc, attn_out, v, x, wo, attn_scale, grad_out, out):
                 ),
             )
             return w_raw
+
+        def load_first_w_half(n):
+            w_half = first.tile([P, PACK, N_TILE], BF16, name="w_first%d" % n)
+            for u in range(2):
+                nc.sync.dma_start(
+                    out=w_half[:, 2 * u : 2 * u + 2, :],
+                    in_=wo[
+                        u * 2 * P : (u + 1) * 2 * P, n * N_TILE : (n + 1) * N_TILE
+                    ].rearrange("(q e) n -> q e n", e=2),
+                )
+            return w_half
 
         def transpose_and_scale_g(g_raw, gs_t, chunk, b):
             words = g_raw[:].bitcast(F32)
@@ -129,16 +149,19 @@ def tile_block_pb_k_kernel(tc, attn_out, v, x, wo, attn_scale, grad_out, out):
                 in_=gs_t[:, b * 2 * K_PASS : (b + 1) * 2 * K_PASS],
             )
 
-        def regroup_w(w_raw):
+        def regroup_w(w_halves):
             w_grp = stage.tile([P, C, PACK], BF16, tag="w_grp", align_bytes=64)
             for copy, cols in (
                 (nc.scalar.copy, slice(0, N_TILE)),
                 (nc.scalar.copy, slice(N_TILE, SCALAR_COLS)),
                 (nc.vector.tensor_copy, slice(SCALAR_COLS, C)),
             ):
+                n = cols.start // N_TILE
                 copy(
                     out=w_grp[:, cols, :].rearrange("p (c i) t -> p c t i", i=4),
-                    in_=w_raw[:, :, cols].rearrange("p t (c i) -> p c t i", i=4),
+                    in_=w_halves[n][:, :, cols.start - n * N_TILE : cols.stop - n * N_TILE].rearrange(
+                        "p t (c i) -> p c t i", i=4
+                    ),
                 )
             return w_grp
 
@@ -173,23 +196,31 @@ def tile_block_pb_k_kernel(tc, attn_out, v, x, wo, attn_scale, grad_out, out):
                     accum_out=ss[:, h * TOKEN_TILES + j : h * TOKEN_TILES + j + 1],
                 )
 
-        for h in range(KV_HEADS):
-            square_v(h)
-
         g_raw_of, w_raw_of, w_grp_of = {}, {}, {}
         for slot in range(-LOAD_AHEAD, PASSES + MX_LAG):
             ahead = slot + LOAD_AHEAD
             preparing = 0 <= slot < PASSES
             multiplying = 0 <= slot - MX_LAG < PASSES
             j, chunk = slot % TOKEN_TILES, slot // TOKEN_TILES
-            if ahead < PASSES:
+            if ahead == 0:
+                w_first = [load_first_w_half(0)[:]]
+                g_raw_of[0] = load_g(0, 0, pieces=2)
+                w_first.append(load_first_w_half(1)[:])
+                w_raw_of[0] = w_first
+            elif ahead < PASSES:
                 g_raw_of[ahead] = load_g(ahead % TOKEN_TILES, ahead // TOKEN_TILES)
-                w_raw_of[ahead] = load_w(ahead)
+                w_raw = load_w(ahead)
+                w_raw_of[ahead] = [w_raw[:, :, n * N_TILE : (n + 1) * N_TILE] for n in range(HALVES)]
+            if ahead == V_SLOT:
+                nc.sync.dma_start(out=v_sb[:].rearrange("p h j d -> p h (j d)"), in_=v_view)
             if preparing:
                 gs_t = stage.tile([P, CHUNK], BF16, tag="gs_t", align_bytes=64)
                 transpose_and_scale_g(g_raw_of[slot], gs_t, chunk, 0)
                 w_grp_of[slot] = regroup_w(w_raw_of[slot])
                 quantise_g(gs_t, j, chunk, 0)
+            if slot == PASSES:
+                for h in range(KV_HEADS):
+                    square_v(h)
             if multiplying:
                 for early in range(EARLY_TILES):
                     multiply(early, slot - MX_LAG, 0)

@@ -140,13 +140,13 @@ def tile_block_pb_k_kernel(tc, attn_out, v, x, wo, attn_scale, grad_out, out):
                 op=ALU.mult,
             )
 
-        def quantise_g(gs_t, j, chunk, b):
-            col = (j * PASSES + chunk * CHUNK_PASSES + 2 * b) * P
-            cols = slice(col, col + 2 * P)
+        def quantise_g(gs_t, j, chunk):
+            col = (j * PASSES + chunk * CHUNK_PASSES) * P
+            cols = slice(col, col + CHUNK_PASSES * P)
             nc.vector.quantize_mx(
                 out=gs_codes[:, cols].bitcast(E5M2_X4),
                 scales=gs_scales[:, cols],
-                in_=gs_t[:, b * 2 * K_PASS : (b + 1) * 2 * K_PASS],
+                in_=gs_t[:],
             )
 
         def regroup_w(w_halves):
@@ -165,13 +165,14 @@ def tile_block_pb_k_kernel(tc, attn_out, v, x, wo, attn_scale, grad_out, out):
                 )
             return w_grp
 
-        def quantise_w(w_grp, c):
-            for n in range(HALVES):
-                cols = slice(c * C + n * N_TILE, c * C + (n + 1) * N_TILE)
+        def quantise_w(w_grp, c, pieces):
+            width = C // pieces
+            for i in range(pieces):
+                cols = slice(c * C + i * width, c * C + (i + 1) * width)
                 nc.vector.quantize_mx(
                     out=w_codes[:, cols].bitcast(E4M3_X4),
                     scales=w_scales[:, cols],
-                    in_=w_grp[:, n * N_TILE : (n + 1) * N_TILE, :].rearrange("p n t -> p (n t)"),
+                    in_=w_grp[:, i * width : (i + 1) * width, :].rearrange("p n t -> p (n t)"),
                 )
 
         def multiply(j, c, n):
@@ -215,24 +216,20 @@ def tile_block_pb_k_kernel(tc, attn_out, v, x, wo, attn_scale, grad_out, out):
                 nc.sync.dma_start(out=v_sb[:].rearrange("p h j d -> p h (j d)"), in_=v_view)
             if preparing:
                 gs_t = stage.tile([P, CHUNK], BF16, tag="gs_t", align_bytes=64)
-                transpose_and_scale_g(g_raw_of[slot], gs_t, chunk, 0)
+                for b in range(2):
+                    transpose_and_scale_g(g_raw_of[slot], gs_t, chunk, b)
                 w_grp_of[slot] = regroup_w(w_raw_of[slot])
-                quantise_g(gs_t, j, chunk, 0)
             if slot == PASSES:
                 for h in range(KV_HEADS):
                     square_v(h)
-            if multiplying:
-                for early in range(EARLY_TILES):
-                    multiply(early, slot - MX_LAG, 0)
-            if preparing:
-                transpose_and_scale_g(g_raw_of[slot], gs_t, chunk, 1)
             if 0 <= slot - 1 < PASSES:
-                quantise_w(w_grp_of[slot - 1], slot - 1)
+                quantise_w(w_grp_of[slot - 1], slot - 1, 1 if slot < PASSES else HALVES)
             if preparing:
-                quantise_g(gs_t, j, chunk, 1)
+                quantise_g(gs_t, j, chunk)
             if multiplying:
-                for early in range(EARLY_TILES):
-                    multiply(early, slot - MX_LAG, 1)
+                for n in range(HALVES):
+                    for early in range(EARLY_TILES):
+                        multiply(early, slot - MX_LAG, n)
 
         for n in range(HALVES):
             acc[(EARLY_TILES, n)] = tp_pool.tile([P, N_TILE], F32, tag="tp", name="acc_late%d" % n)

@@ -31,7 +31,6 @@ BANK_HEADS = N_TILE // HEAD_DIM
 EARLY_TILES = 3
 LOAD_AHEAD = 3
 MX_LAG = 3
-V_SLOT = 8
 SCALAR_COLS = 768
 
 FLOPS = 2 * TOKENS * D * C
@@ -47,7 +46,6 @@ def tile_block_pb_k_kernel(tc, attn_out, v, x, wo, attn_scale, grad_out, out):
     with ExitStack() as ctx:
         const = ctx.enter_context(tc.tile_pool(name="const", bufs=1))
         keep = ctx.enter_context(tc.tile_pool(name="keep", bufs=1))
-        first = ctx.enter_context(tc.tile_pool(name="first", bufs=1))
         raw = ctx.enter_context(tc.tile_pool(name="raw", bufs=LOAD_AHEAD + 1))
         stage = ctx.enter_context(tc.tile_pool(name="stage", bufs=3))
         tail = ctx.enter_context(tc.tile_pool(name="tail", bufs=3))
@@ -60,18 +58,23 @@ def tile_block_pb_k_kernel(tc, attn_out, v, x, wo, attn_scale, grad_out, out):
 
         v_sb = const.tile([P, KV_HEADS, TOKEN_TILES, HEAD_DIM], BF16)
 
-        sc_rows = const.tile([P, 2 * P], BF16)
+        sc_rows = const.tile([P, K_PASS], BF16)
         nc.vector.memset(sc_rows[:], 0.0)
         nc.sync.dma_start(
-            out=sc_rows[0 : D // (2 * P), :], in_=attn_scale.rearrange("(r w) -> r w", w=2 * P)
+            out=sc_rows[0:PASSES, :], in_=attn_scale.rearrange("(r w) -> r w", w=K_PASS)
         )
+        nc.scalar.dma_start(out=v_sb[:].rearrange("p h j d -> p h (j d)"), in_=v_view)
         table = const.tile([P, 2], F32)
         nc.vector.memset(table[:, 0:1], 0.0)
         nc.scalar.copy(out=table[:, 1:2], in_=table[:, 0:1])
         sc_ps = tp_pool.tile([P, PACK, P], F32, tag="tp")
-        nc.tensor.transpose(sc_ps[:, 0, :], sc_rows[:].bitcast(F32), ident[:])
+        for u in range(2):
+            nc.tensor.transpose(sc_ps[:, u, :], sc_rows[:].bitcast(F32)[:, u::2], ident[:])
         sc_t = const.tile([P, PASSES * PACK], BF16)
-        nc.vector.tensor_copy(out=sc_t[:].bitcast(F32), in_=sc_ps[:, 0, 0 : PASSES * 2])
+        nc.vector.tensor_copy(
+            out=sc_t[:].bitcast(F32).rearrange("p (c u) -> p c u", u=2),
+            in_=sc_ps[:, 0:2, 0:PASSES].rearrange("p u c -> p c u"),
+        )
 
         gs_codes = keep.tile([P, TOKEN_TILES * PASSES * P], U32, align_bytes=64)
         gs_scales = keep.tile([P, TOKEN_TILES * PASSES * P], U8, align_bytes=64)
@@ -86,44 +89,28 @@ def tile_block_pb_k_kernel(tc, attn_out, v, x, wo, attn_scale, grad_out, out):
             for j in range(EARLY_TILES):
                 acc[(j, n)] = acc_pool.tile([P, N_TILE], F32, name="acc%d%d" % (j, n))
 
-        def load_g(j, chunk, pieces=1):
+        def load_g(j, chunk):
             g_raw = raw.tile([P, CHUNK], BF16, tag="g_raw")
-            width = CHUNK // pieces
-            for i in range(pieces):
-                k0 = chunk * CHUNK + i * width
-                nc.sync.dma_start(
-                    out=g_raw[:, i * width : (i + 1) * width], in_=g_view[:, j, k0 : k0 + width]
-                )
+            nc.sync.dma_start(out=g_raw[:], in_=g_view[:, j, chunk * CHUNK : (chunk + 1) * CHUNK])
             return g_raw
 
         def load_w(c):
             w_raw = raw.tile([P, PACK, C], BF16, tag="w_raw")
             nc.sync.dma_start(
-                out=w_raw[:].rearrange("p (u e) n -> p u (e n)", u=2),
-                in_=wo[c * K_PASS : (c + 1) * K_PASS, :].rearrange(
-                    "(u q e) n -> q u (e n)", u=2, e=2
-                ),
+                out=w_raw[:],
+                in_=wo[c * K_PASS : (c + 1) * K_PASS, :].rearrange("(q t) n -> q t n", t=PACK),
             )
             return w_raw
-
-        def load_first_w_half(n):
-            w_half = first.tile([P, PACK, N_TILE], BF16, name="w_first%d" % n)
-            for u in range(2):
-                nc.sync.dma_start(
-                    out=w_half[:, 2 * u : 2 * u + 2, :],
-                    in_=wo[
-                        u * 2 * P : (u + 1) * 2 * P, n * N_TILE : (n + 1) * N_TILE
-                    ].rearrange("(q e) n -> q e n", e=2),
-                )
-            return w_half
 
         def transpose_and_scale_g(g_raw, gs_t, chunk, b):
             words = g_raw[:].bitcast(F32)
             xt = tp_pool.tile([P, PACK, P], F32, tag="tp")
             for c in range(2):
                 for u in range(2):
-                    w0 = ((2 * b + c) * 2 + u) * P
-                    nc.tensor.transpose(xt[:, 2 * u + c, :], words[:, w0 : w0 + P], ident[:])
+                    w0 = (2 * b + c) * 2 * P
+                    nc.tensor.transpose(
+                        xt[:, 2 * u + c, :], words[:, w0 + u : w0 + 2 * P : 2], ident[:]
+                    )
             first = (chunk * CHUNK_PASSES + 2 * b) * PACK
             nc.vector.tensor_tensor(
                 out=gs_t[:, b * 2 * K_PASS : (b + 1) * 2 * K_PASS].rearrange(
@@ -197,31 +184,24 @@ def tile_block_pb_k_kernel(tc, attn_out, v, x, wo, attn_scale, grad_out, out):
                     accum_out=ss[:, h * TOKEN_TILES + j : h * TOKEN_TILES + j + 1],
                 )
 
+        for h in range(KV_HEADS):
+            square_v(h)
+
         g_raw_of, w_raw_of, w_grp_of = {}, {}, {}
         for slot in range(-LOAD_AHEAD, PASSES + MX_LAG):
             ahead = slot + LOAD_AHEAD
             preparing = 0 <= slot < PASSES
             multiplying = 0 <= slot - MX_LAG < PASSES
             j, chunk = slot % TOKEN_TILES, slot // TOKEN_TILES
-            if ahead == 0:
-                w_first = [load_first_w_half(0)[:]]
-                g_raw_of[0] = load_g(0, 0, pieces=2)
-                w_first.append(load_first_w_half(1)[:])
-                w_raw_of[0] = w_first
-            elif ahead < PASSES:
+            if ahead < PASSES:
                 g_raw_of[ahead] = load_g(ahead % TOKEN_TILES, ahead // TOKEN_TILES)
                 w_raw = load_w(ahead)
                 w_raw_of[ahead] = [w_raw[:, :, n * N_TILE : (n + 1) * N_TILE] for n in range(HALVES)]
-            if ahead == V_SLOT:
-                nc.sync.dma_start(out=v_sb[:].rearrange("p h j d -> p h (j d)"), in_=v_view)
             if preparing:
                 gs_t = stage.tile([P, CHUNK], BF16, tag="gs_t", align_bytes=64)
                 for b in range(2):
                     transpose_and_scale_g(g_raw_of[slot], gs_t, chunk, b)
                 w_grp_of[slot] = regroup_w(w_raw_of[slot])
-            if slot == PASSES:
-                for h in range(KV_HEADS):
-                    square_v(h)
             if 0 <= slot - 1 < PASSES:
                 quantise_w(w_grp_of[slot - 1], slot - 1, 1 if slot < PASSES else HALVES)
             if preparing:

@@ -30,8 +30,11 @@ HALVES = C // N_TILE
 BANK_HEADS = N_TILE // HEAD_DIM
 EARLY_TILES = 3
 LOAD_AHEAD = 3
-MX_LAG = 3
-SCALAR_COLS = 768
+SCALAR_COLS = (576, 768, 768)
+CHUNKS_OF = (2, 1, 1, 1, 1, 1, 1, 1, 1, 1, 1, 1, 1, 1, 1, 0)
+PASSES_IN = ((), (), (0,), (1,), (2,), (3,), (4,), (5,), (6,), (7,), (8,), (9,), (10,), (11,), (12,), (13,), (14, 15))
+FINISH_LAG = 1
+LATE_IN = {15: 8}
 
 FLOPS = 2 * TOKENS * D * C
 BYTES = 2 * (D * C + TOKENS * D + KV_HEADS * TOKENS * HEAD_DIM + D) + 4 * TOKENS * C
@@ -46,6 +49,7 @@ def tile_block_pb_k_kernel(tc, attn_out, v, x, wo, attn_scale, grad_out, out):
     with ExitStack() as ctx:
         const = ctx.enter_context(tc.tile_pool(name="const", bufs=1))
         keep = ctx.enter_context(tc.tile_pool(name="keep", bufs=1))
+        raw_g = ctx.enter_context(tc.tile_pool(name="raw_g", bufs=LOAD_AHEAD + 2))
         raw = ctx.enter_context(tc.tile_pool(name="raw", bufs=LOAD_AHEAD + 1))
         stage = ctx.enter_context(tc.tile_pool(name="stage", bufs=3))
         tail = ctx.enter_context(tc.tile_pool(name="tail", bufs=3))
@@ -90,7 +94,7 @@ def tile_block_pb_k_kernel(tc, attn_out, v, x, wo, attn_scale, grad_out, out):
                 acc[(j, n)] = acc_pool.tile([P, N_TILE], F32, name="acc%d%d" % (j, n))
 
         def load_g(j, chunk):
-            g_raw = raw.tile([P, CHUNK], BF16, tag="g_raw")
+            g_raw = raw_g.tile([P, CHUNK], BF16, tag="g_raw")
             nc.sync.dma_start(out=g_raw[:], in_=g_view[:, j, chunk * CHUNK : (chunk + 1) * CHUNK])
             return g_raw
 
@@ -136,13 +140,15 @@ def tile_block_pb_k_kernel(tc, attn_out, v, x, wo, attn_scale, grad_out, out):
                 in_=gs_t[:],
             )
 
-        def regroup_w(w_halves):
+        def regroup_w(w_halves, scalar_cols):
             w_grp = stage.tile([P, C, PACK], BF16, tag="w_grp", align_bytes=64)
             for copy, cols in (
                 (nc.scalar.copy, slice(0, N_TILE)),
-                (nc.scalar.copy, slice(N_TILE, SCALAR_COLS)),
-                (nc.vector.tensor_copy, slice(SCALAR_COLS, C)),
+                (nc.scalar.copy, slice(N_TILE, scalar_cols)),
+                (nc.vector.tensor_copy, slice(scalar_cols, C)),
             ):
+                if cols.start >= cols.stop:
+                    continue
                 n = cols.start // N_TILE
                 copy(
                     out=w_grp[:, cols, :].rearrange("p (c i) t -> p c t i", i=4),
@@ -187,35 +193,69 @@ def tile_block_pb_k_kernel(tc, attn_out, v, x, wo, attn_scale, grad_out, out):
         for h in range(KV_HEADS):
             square_v(h)
 
+        late_passes = [(c, n) for n in range(HALVES) for c in range(PASSES)]
+
+        def multiply_early(c, n):
+            for early in range(EARLY_TILES):
+                multiply(early, c, n)
+
+        def multiply_late(count):
+            for c, n in late_passes[:count]:
+                multiply(EARLY_TILES, c, n)
+            late_passes[:count] = []
+
         g_raw_of, w_raw_of, w_grp_of = {}, {}, {}
-        for slot in range(-LOAD_AHEAD, PASSES + MX_LAG):
+        chunks_in = {}
+        for slot in range(PASSES):
+            start = sum(CHUNKS_OF[:slot])
+            chunks_in[slot] = list(range(start, start + CHUNKS_OF[slot]))
+        last_chunk_slot = max(s for s in chunks_in if chunks_in[s])
+        for slot in range(-LOAD_AHEAD, PASSES + 1):
             ahead = slot + LOAD_AHEAD
             preparing = 0 <= slot < PASSES
-            multiplying = 0 <= slot - MX_LAG < PASSES
-            j, chunk = slot % TOKEN_TILES, slot // TOKEN_TILES
             if ahead < PASSES:
-                g_raw_of[ahead] = load_g(ahead % TOKEN_TILES, ahead // TOKEN_TILES)
+                for i in chunks_in[ahead]:
+                    g_raw_of[i] = load_g(i % TOKEN_TILES, i // TOKEN_TILES)
                 w_raw = load_w(ahead)
                 w_raw_of[ahead] = [w_raw[:, :, n * N_TILE : (n + 1) * N_TILE] for n in range(HALVES)]
-            if preparing:
-                gs_t = stage.tile([P, CHUNK], BF16, tag="gs_t", align_bytes=64)
-                for b in range(2):
-                    transpose_and_scale_g(g_raw_of[slot], gs_t, chunk, b)
-                w_grp_of[slot] = regroup_w(w_raw_of[slot])
-            if 0 <= slot - 1 < PASSES:
-                quantise_w(w_grp_of[slot - 1], slot - 1, 1 if slot < PASSES else HALVES)
-            if preparing:
-                quantise_g(gs_t, j, chunk)
-            if multiplying:
-                for n in range(HALVES):
-                    for early in range(EARLY_TILES):
-                        multiply(early, slot - MX_LAG, n)
+            if slot < 0:
+                continue
+            chunks = chunks_in.get(slot, [])
+            scaled = []
 
-        for n in range(HALVES):
-            acc[(EARLY_TILES, n)] = tp_pool.tile([P, N_TILE], F32, tag="tp", name="acc_late%d" % n)
-        for n in range(HALVES):
-            for c in range(PASSES):
-                multiply(EARLY_TILES, c, n)
+            def scale_next():
+                if len(scaled) < len(chunks):
+                    i = chunks[len(scaled)]
+                    gs_t = stage.tile([P, CHUNK], BF16, tag="gs_t", align_bytes=64)
+                    for b in range(2):
+                        transpose_and_scale_g(g_raw_of[i], gs_t, i // TOKEN_TILES, b)
+                    scaled.append((gs_t, i))
+
+            passes = PASSES_IN[slot]
+            scale_next()
+            if preparing:
+                w_grp_of[slot] = regroup_w(w_raw_of[slot], SCALAR_COLS[len(chunks)])
+            if slot == last_chunk_slot + 1:
+                for n in range(HALVES):
+                    acc[(EARLY_TILES, n)] = tp_pool.tile(
+                        [P, N_TILE], F32, tag="tp", name="acc_late%d" % n
+                    )
+            if slot == PASSES:
+                quantise_w(w_grp_of[slot - 1], slot - 1, HALVES)
+            elif slot > 0:
+                quantise_w(w_grp_of[slot - 1], slot - 1, 1)
+            for c in passes[:1]:
+                multiply_early(c, 0)
+            scale_next()
+            for gs_t, i in scaled:
+                quantise_g(gs_t, i % TOKEN_TILES, i // TOKEN_TILES)
+            for c in passes[:1]:
+                multiply_early(c, 1)
+            for c in passes[1:]:
+                multiply_early(c, 0)
+                multiply_early(c, 1)
+            multiply_late(LATE_IN.get(slot, 0))
+        multiply_late(len(late_passes))
 
         neg_ss = const.tile([P, KV_HEADS, TOKEN_TILES], F32)
         neg_inv = const.tile([P, KV_HEADS, TOKEN_TILES], F32)
@@ -265,10 +305,12 @@ def tile_block_pb_k_kernel(tc, attn_out, v, x, wo, attn_scale, grad_out, out):
                 out=out_view[:, j, n * BANK_HEADS : (n + 1) * BANK_HEADS, :], in_=res[:]
             )
 
-        banks = [(j, n) for j in range(TOKEN_TILES) for n in range(HALVES)]
+        banks = [(j, n) for n in range(HALVES) for j in range(EARLY_TILES)]
+        banks += [(EARLY_TILES, n) for n in range(HALVES)]
         coefs = {}
         for b, bank in enumerate(banks):
             coefs[bank] = start_projection(*bank)
-            if b > 0:
-                finish_projection(*banks[b - 1], coefs[banks[b - 1]])
-        finish_projection(*banks[-1], coefs[banks[-1]])
+            if b >= FINISH_LAG:
+                finish_projection(*banks[b - FINISH_LAG], coefs[banks[b - FINISH_LAG]])
+        for bank in banks[-FINISH_LAG:]:
+            finish_projection(*bank, coefs[bank])

@@ -30,11 +30,12 @@ HALVES = C // N_TILE
 BANK_HEADS = N_TILE // HEAD_DIM
 EARLY_TILES = 3
 LOAD_AHEAD = 3
-SCALAR_COLS = (576, 768, 768)
+SCALAR_COLS = (608, 784, 832)
 CHUNKS_OF = (2, 1, 1, 1, 1, 1, 1, 1, 1, 1, 1, 1, 1, 1, 1, 0)
 PASSES_IN = ((), (), (0,), (1,), (2,), (3,), (4,), (5,), (6,), (7,), (8,), (9,), (10,), (11,), (12,), (13,), (14, 15))
 FINISH_LAG = 1
-LATE_IN = {15: 8}
+LATE_BEFORE = {15: 8}
+LATE_IN = {15: 2}
 
 FLOPS = 2 * TOKENS * D * C
 BYTES = 2 * (D * C + TOKENS * D + KV_HEADS * TOKENS * HEAD_DIM + D) + 4 * TOKENS * C
@@ -244,6 +245,7 @@ def tile_block_pb_k_kernel(tc, attn_out, v, x, wo, attn_scale, grad_out, out):
                 quantise_w(w_grp_of[slot - 1], slot - 1, HALVES)
             elif slot > 0:
                 quantise_w(w_grp_of[slot - 1], slot - 1, 1)
+            multiply_late(LATE_BEFORE.get(slot, 0))
             for c in passes[:1]:
                 multiply_early(c, 0)
             scale_next()

@@ -114,7 +114,9 @@ def tile_block_pb_k_kernel(tc, attn_out, v, x, wo, attn_scale, grad_out, out):
                 for u in range(2):
                     w0 = (2 * b + c) * 2 * P
                     nc.tensor.transpose(
-                        xt[:, 2 * u + c, :], words[:, w0 + u : w0 + 2 * P : 2], ident[:]
+                        xt[:, 2 * c : 2 * c + 2, :].rearrange("p u r -> p (u r)")[:, u::2],
+                        words[:, w0 + u : w0 + 2 * P : 2],
+                        ident[:],
                     )
             first = (chunk * CHUNK_PASSES + 2 * b) * PACK
             nc.vector.tensor_tensor(
@@ -124,7 +126,7 @@ def tile_block_pb_k_kernel(tc, attn_out, v, x, wo, attn_scale, grad_out, out):
                 in0=xt[:]
                 .rearrange("p s r -> p (s r)")
                 .bitcast(BF16)
-                .rearrange("p (u c r e) -> p c r u e", u=2, c=2, e=2),
+                .rearrange("p (c r u e) -> p c r u e", u=2, c=2, e=2),
                 in1=sc_t[:, first : first + 2 * PACK]
                 .rearrange("p (c u e) -> p c u e", c=2, u=2)
                 .unsqueeze(2)
@@ -234,6 +236,11 @@ def tile_block_pb_k_kernel(tc, attn_out, v, x, wo, attn_scale, grad_out, out):
 
             passes = PASSES_IN[slot]
             scale_next()
+            if slot == 0:
+                while len(scaled) < len(chunks):
+                    scale_next()
+                for gs_t, i in scaled:
+                    quantise_g(gs_t, i % TOKEN_TILES, i // TOKEN_TILES)
             if preparing:
                 w_grp_of[slot] = regroup_w(w_raw_of[slot], SCALAR_COLS[len(chunks)])
             if slot == last_chunk_slot + 1:
@@ -249,7 +256,7 @@ def tile_block_pb_k_kernel(tc, attn_out, v, x, wo, attn_scale, grad_out, out):
             for c in passes[:1]:
                 multiply_early(c, 0)
             scale_next()
-            for gs_t, i in scaled:
+            for gs_t, i in scaled if slot > 0 else ():
                 quantise_g(gs_t, i % TOKEN_TILES, i // TOKEN_TILES)
             for c in passes[:1]:
                 multiply_early(c, 1)
@@ -292,7 +299,7 @@ def tile_block_pb_k_kernel(tc, attn_out, v, x, wo, attn_scale, grad_out, out):
                 )
             return coef
 
-        def finish_projection(j, n, coef):
+        def finish_projection(j, n, coef, pieces=1):
             res = tail.tile([P, BANK_HEADS, HEAD_DIM], F32, tag="res")
             for q in range(BANK_HEADS):
                 nc.vector.scalar_tensor_tensor(
@@ -303,9 +310,13 @@ def tile_block_pb_k_kernel(tc, attn_out, v, x, wo, attn_scale, grad_out, out):
                     op0=ALU.mult,
                     op1=ALU.add,
                 )
-            nc.sync.dma_start(
-                out=out_view[:, j, n * BANK_HEADS : (n + 1) * BANK_HEADS, :], in_=res[:]
-            )
+                width = BANK_HEADS // pieces
+                if (q + 1) % width == 0:
+                    q0 = q + 1 - width
+                    nc.sync.dma_start(
+                        out=out_view[:, j, n * BANK_HEADS + q0 : n * BANK_HEADS + q + 1, :],
+                        in_=res[:, q0 : q + 1, :],
+                    )
 
         banks = [(j, n) for n in range(HALVES) for j in range(EARLY_TILES)]
         banks += [(EARLY_TILES, n) for n in range(HALVES)]
@@ -315,4 +326,4 @@ def tile_block_pb_k_kernel(tc, attn_out, v, x, wo, attn_scale, grad_out, out):
             if b >= FINISH_LAG:
                 finish_projection(*banks[b - FINISH_LAG], coefs[banks[b - FINISH_LAG]])
         for bank in banks[-FINISH_LAG:]:
-            finish_projection(*bank, coefs[bank])
+            finish_projection(*bank, coefs[bank], pieces=2)

@@ -35,7 +35,7 @@ CHUNKS_OF = (2, 1, 1, 1, 1, 1, 1, 1, 1, 1, 1, 1, 1, 1, 1, 0)
 PASSES_IN = ((), (), (0,), (1,), (2,), (3,), (4,), (5,), (6,), (7,), (8,), (9,), (10,), (11,), (12,), (13,), (14, 15))
 FINISH_LAG = 1
 LATE_BEFORE = {15: 8}
-LATE_IN = {15: 2}
+LATE_IN = {15: 1}
 
 FLOPS = 2 * TOKENS * D * C
 BYTES = 2 * (D * C + TOKENS * D + KV_HEADS * TOKENS * HEAD_DIM + D) + 4 * TOKENS * C
@@ -68,7 +68,6 @@ def tile_block_pb_k_kernel(tc, attn_out, v, x, wo, attn_scale, grad_out, out):
         nc.sync.dma_start(
             out=sc_rows[0:PASSES, :], in_=attn_scale.rearrange("(r w) -> r w", w=K_PASS)
         )
-        nc.scalar.dma_start(out=v_sb[:].rearrange("p h j d -> p h (j d)"), in_=v_view)
         table = const.tile([P, 2], F32)
         nc.vector.memset(table[:, 0:1], 0.0)
         nc.scalar.copy(out=table[:, 1:2], in_=table[:, 0:1])
@@ -87,7 +86,7 @@ def tile_block_pb_k_kernel(tc, attn_out, v, x, wo, attn_scale, grad_out, out):
         w_scales = keep.tile([P, PASSES * C], U8, align_bytes=64)
 
         sq = const.tile([P, KV_HEADS, TOKEN_TILES, HEAD_DIM], BF16)
-        ss = const.tile([P, KV_HEADS * TOKEN_TILES], F32)
+        ss = [const.tile([P, 2 * TOKEN_TILES], F32, name="ss%d" % n) for n in range(HALVES)]
 
         acc = {}
         for n in range(HALVES):
@@ -190,11 +189,8 @@ def tile_block_pb_k_kernel(tc, attn_out, v, x, wo, attn_scale, grad_out, out):
                     out=sq[:, h, j, :],
                     in_=v_sb[:, h, j, :],
                     func=ACT.Square,
-                    accum_out=ss[:, h * TOKEN_TILES + j : h * TOKEN_TILES + j + 1],
+                    accum_out=ss[h // 2][:, (h % 2) * TOKEN_TILES + j : (h % 2) * TOKEN_TILES + j + 1],
                 )
-
-        for h in range(KV_HEADS):
-            square_v(h)
 
         late_passes = [(c, n) for n in range(HALVES) for c in range(PASSES)]
 
@@ -221,6 +217,8 @@ def tile_block_pb_k_kernel(tc, attn_out, v, x, wo, attn_scale, grad_out, out):
                     g_raw_of[i] = load_g(i % TOKEN_TILES, i // TOKEN_TILES)
                 w_raw = load_w(ahead)
                 w_raw_of[ahead] = [w_raw[:, :, n * N_TILE : (n + 1) * N_TILE] for n in range(HALVES)]
+            if ahead == PASSES - 1:
+                nc.sync.dma_start(out=v_sb[:].rearrange("p h j d -> p h (j d)"), in_=v_view)
             if slot < 0:
                 continue
             chunks = chunks_in.get(slot, [])
@@ -248,6 +246,9 @@ def tile_block_pb_k_kernel(tc, attn_out, v, x, wo, attn_scale, grad_out, out):
                     acc[(EARLY_TILES, n)] = tp_pool.tile(
                         [P, N_TILE], F32, tag="tp", name="acc_late%d" % n
                     )
+            if slot == PASSES - 1:
+                for h in range(2):
+                    square_v(h)
             if slot == PASSES:
                 quantise_w(w_grp_of[slot - 1], slot - 1, HALVES)
             elif slot > 0:
@@ -266,17 +267,20 @@ def tile_block_pb_k_kernel(tc, attn_out, v, x, wo, attn_scale, grad_out, out):
             multiply_late(LATE_IN.get(slot, 0))
         multiply_late(len(late_passes))
 
-        neg_ss = const.tile([P, KV_HEADS, TOKEN_TILES], F32)
-        neg_inv = const.tile([P, KV_HEADS, TOKEN_TILES], F32)
-        nc.vector.tensor_scalar(
-            out=neg_ss[:].rearrange("p h j -> p (h j)"),
-            in0=ss[:],
-            scalar1=1e-24,
-            scalar2=-1.0,
-            op0=ALU.max,
-            op1=ALU.mult,
-        )
-        nc.vector.reciprocal(out=neg_inv[:], in_=neg_ss[:])
+        neg_inv = {}
+
+        def invert_norms(n):
+            neg_ss = const.tile([P, 2, TOKEN_TILES], F32, name="neg_ss%d" % n)
+            neg_inv[n] = const.tile([P, 2, TOKEN_TILES], F32, name="neg_inv%d" % n)
+            nc.vector.tensor_scalar(
+                out=neg_ss[:].rearrange("p h j -> p (h j)"),
+                in0=ss[n][:],
+                scalar1=1e-24,
+                scalar2=-1.0,
+                op0=ALU.max,
+                op1=ALU.mult,
+            )
+            nc.vector.reciprocal(out=neg_inv[n][:], in_=neg_ss[:])
 
         def start_projection(j, n):
             prod = tail.tile([P, BANK_HEADS, HEAD_DIM], F32, tag="prod")
@@ -288,13 +292,15 @@ def tile_block_pb_k_kernel(tc, attn_out, v, x, wo, attn_scale, grad_out, out):
                 .to_broadcast([P, 2, GROUP, HEAD_DIM]),
                 op=ALU.mult,
             )
+            if n not in neg_inv:
+                invert_norms(n)
             coef = tail.tile([P, BANK_HEADS], F32, tag="coef")
             for q in range(BANK_HEADS):
                 nc.scalar.activation(
                     out=prod[:, q, :],
                     in_=prod[:, q, :],
                     func=ACT.Copy,
-                    scale=neg_inv[:, 2 * n + q // GROUP, j : j + 1],
+                    scale=neg_inv[n][:, q // GROUP, j : j + 1],
                     accum_out=coef[:, q : q + 1],
                 )
             return coef
@@ -323,6 +329,8 @@ def tile_block_pb_k_kernel(tc, attn_out, v, x, wo, attn_scale, grad_out, out):
         coefs = {}
         for b, bank in enumerate(banks):
             coefs[bank] = start_projection(*bank)
+            if b < 2:
+                square_v(2 + b)
             if b >= FINISH_LAG:
                 finish_projection(*banks[b - FINISH_LAG], coefs[banks[b - FINISH_LAG]])
         for bank in banks[-FINISH_LAG:]:

@@ -33,6 +33,7 @@ LOAD_AHEAD = 3
 SCALAR_COLS = (608, 784, 832)
 CHUNKS_OF = (2, 1, 1, 1, 1, 1, 1, 1, 1, 1, 1, 1, 1, 1, 1, 0)
 PASSES_IN = ((), (), (0,), (1,), (2,), (3,), (4,), (5,), (6,), (7,), (8,), (9,), (10,), (11,), (12,), (13,), (14, 15))
+SQUARES_FIRST = 3
 FINISH_LAG = 1
 LATE_BEFORE = {15: 8}
 LATE_IN = {15: 1}
@@ -63,6 +64,13 @@ def tile_block_pb_k_kernel(tc, attn_out, v, x, wo, attn_scale, grad_out, out):
 
         v_sb = const.tile([P, KV_HEADS, TOKEN_TILES, HEAD_DIM], BF16)
 
+        def load_g(j, chunk):
+            g_raw = raw_g.tile([P, CHUNK], BF16, tag="g_raw")
+            nc.sync.dma_start(out=g_raw[:], in_=g_view[:, j, chunk * CHUNK : (chunk + 1) * CHUNK])
+            return g_raw
+
+        first_g = load_g(0, 0)
+
         sc_rows = const.tile([P, K_PASS], BF16)
         nc.vector.memset(sc_rows[:], 0.0)
         nc.sync.dma_start(
@@ -92,11 +100,6 @@ def tile_block_pb_k_kernel(tc, attn_out, v, x, wo, attn_scale, grad_out, out):
         for n in range(HALVES):
             for j in range(EARLY_TILES):
                 acc[(j, n)] = acc_pool.tile([P, N_TILE], F32, name="acc%d%d" % (j, n))
-
-        def load_g(j, chunk):
-            g_raw = raw_g.tile([P, CHUNK], BF16, tag="g_raw")
-            nc.sync.dma_start(out=g_raw[:], in_=g_view[:, j, chunk * CHUNK : (chunk + 1) * CHUNK])
-            return g_raw
 
         def load_w(c):
             w_raw = raw.tile([P, PACK, C], BF16, tag="w_raw")
@@ -214,7 +217,10 @@ def tile_block_pb_k_kernel(tc, attn_out, v, x, wo, attn_scale, grad_out, out):
             preparing = 0 <= slot < PASSES
             if ahead < PASSES:
                 for i in chunks_in[ahead]:
-                    g_raw_of[i] = load_g(i % TOKEN_TILES, i // TOKEN_TILES)
+                    if i == 0:
+                        g_raw_of[i] = first_g
+                    else:
+                        g_raw_of[i] = load_g(i % TOKEN_TILES, i // TOKEN_TILES)
                 w_raw = load_w(ahead)
                 w_raw_of[ahead] = [w_raw[:, :, n * N_TILE : (n + 1) * N_TILE] for n in range(HALVES)]
             if ahead == PASSES - 1:
@@ -247,7 +253,7 @@ def tile_block_pb_k_kernel(tc, attn_out, v, x, wo, attn_scale, grad_out, out):
                         [P, N_TILE], F32, tag="tp", name="acc_late%d" % n
                     )
             if slot == PASSES - 1:
-                for h in range(2):
+                for h in range(SQUARES_FIRST):
                     square_v(h)
             if slot == PASSES:
                 quantise_w(w_grp_of[slot - 1], slot - 1, HALVES)
@@ -267,20 +273,24 @@ def tile_block_pb_k_kernel(tc, attn_out, v, x, wo, attn_scale, grad_out, out):
             multiply_late(LATE_IN.get(slot, 0))
         multiply_late(len(late_passes))
 
-        neg_inv = {}
+        neg_ss = [const.tile([P, 2, TOKEN_TILES], F32, name="neg_ss%d" % n) for n in range(HALVES)]
+        neg_inv = [const.tile([P, 2, TOKEN_TILES], F32, name="neg_inv%d" % n) for n in range(HALVES)]
 
-        def invert_norms(n):
-            neg_ss = const.tile([P, 2, TOKEN_TILES], F32, name="neg_ss%d" % n)
-            neg_inv[n] = const.tile([P, 2, TOKEN_TILES], F32, name="neg_inv%d" % n)
+        def negate_norms(n):
             nc.vector.tensor_scalar(
-                out=neg_ss[:].rearrange("p h j -> p (h j)"),
+                out=neg_ss[n][:].rearrange("p h j -> p (h j)"),
                 in0=ss[n][:],
                 scalar1=1e-24,
                 scalar2=-1.0,
                 op0=ALU.max,
                 op1=ALU.mult,
             )
-            nc.vector.reciprocal(out=neg_inv[n][:], in_=neg_ss[:])
+
+        def invert_norms(n):
+            nc.vector.reciprocal(out=neg_inv[n][:], in_=neg_ss[n][:])
+
+        banks = [(j, n) for n in range(HALVES) for j in range(EARLY_TILES)]
+        banks += [(EARLY_TILES, n) for n in range(HALVES)]
 
         def start_projection(j, n):
             prod = tail.tile([P, BANK_HEADS, HEAD_DIM], F32, tag="prod")
@@ -292,7 +302,7 @@ def tile_block_pb_k_kernel(tc, attn_out, v, x, wo, attn_scale, grad_out, out):
                 .to_broadcast([P, 2, GROUP, HEAD_DIM]),
                 op=ALU.mult,
             )
-            if n not in neg_inv:
+            if (j, n) == banks[0]:
                 invert_norms(n)
             coef = tail.tile([P, BANK_HEADS], F32, tag="coef")
             for q in range(BANK_HEADS):
@@ -324,14 +334,17 @@ def tile_block_pb_k_kernel(tc, attn_out, v, x, wo, attn_scale, grad_out, out):
                         in_=res[:, q0 : q + 1, :],
                     )
 
-        banks = [(j, n) for n in range(HALVES) for j in range(EARLY_TILES)]
-        banks += [(EARLY_TILES, n) for n in range(HALVES)]
         coefs = {}
+        negate_norms(0)
         for b, bank in enumerate(banks):
             coefs[bank] = start_projection(*bank)
-            if b < 2:
-                square_v(2 + b)
+            if b < KV_HEADS - SQUARES_FIRST:
+                square_v(SQUARES_FIRST + b)
+            if b == EARLY_TILES - 1:
+                negate_norms(1)
             if b >= FINISH_LAG:
                 finish_projection(*banks[b - FINISH_LAG], coefs[banks[b - FINISH_LAG]])
+            if b == EARLY_TILES - 1:
+                invert_norms(1)
         for bank in banks[-FINISH_LAG:]:
             finish_projection(*bank, coefs[bank], pieces=2)

from contextlib import ExitStack

import concourse.mybir as mybir
from concourse.masks import make_identity

BF16 = mybir.dt.bfloat16
F32 = mybir.dt.float32
U32 = mybir.dt.uint32
U8 = mybir.dt.uint8
E4M3_X4 = mybir.dt.float8_e4m3fn_x4
E5M2_X4 = mybir.dt.float8_e5m2_x4
ALU = mybir.AluOpType
ACT = mybir.ActivationFunctionType

P = 128
TOKENS = 512
D = 8192
KV_HEADS = 4
GROUP = 2
HEAD_DIM = 128
C = KV_HEADS * GROUP * HEAD_DIM
PACK = 4
K_PASS = P * PACK
PASSES = D // K_PASS
TOKEN_TILES = TOKENS // P
CHUNK_PASSES = 4
CHUNK = CHUNK_PASSES * K_PASS
N_TILE = 512
HALVES = C // N_TILE
BANK_HEADS = N_TILE // HEAD_DIM
EARLY_TILES = 3
LOAD_AHEAD = 3
SCALAR_COLS = (608, 784, 832)
CHUNKS_OF = (2, 1, 1, 1, 1, 1, 1, 1, 1, 1, 1, 1, 1, 1, 1, 0)
PASSES_IN = ((), (), (0,), (1,), (2,), (3,), (4,), (5,), (6,), (7,), (8,), (9,), (10,), (11,), (12,), (13,), (14, 15))
SQUARES_FIRST = 3
FINISH_LAG = 1
LATE_BEFORE = {15: 8}
LATE_IN = {15: 1}

FLOPS = 2 * TOKENS * D * C
BYTES = 2 * (D * C + TOKENS * D + KV_HEADS * TOKENS * HEAD_DIM + D) + 4 * TOKENS * C


def tile_block_pb_k_kernel(tc, attn_out, v, x, wo, attn_scale, grad_out, out):
    nc = tc.nc
    g_view = grad_out[0].rearrange("(p j) k -> p j k", j=TOKEN_TILES)
    v_view = v[0].rearrange("h (p j) d -> p h (j d)", j=TOKEN_TILES)
    out_view = out[0].rearrange("h g (p j) d -> p j (h g) d", j=TOKEN_TILES)

    with ExitStack() as ctx:
        const = ctx.enter_context(tc.tile_pool(name="const", bufs=1))
        keep = ctx.enter_context(tc.tile_pool(name="keep", bufs=1))
        raw_g = ctx.enter_context(tc.tile_pool(name="raw_g", bufs=LOAD_AHEAD + 2))
        raw = ctx.enter_context(tc.tile_pool(name="raw", bufs=LOAD_AHEAD + 1))
        stage = ctx.enter_context(tc.tile_pool(name="stage", bufs=3))
        tail = ctx.enter_context(tc.tile_pool(name="tail", bufs=3))
        acc_pool = ctx.enter_context(tc.psum_pool(name="acc", bufs=1))
        tp_pool = ctx.enter_context(tc.psum_pool(name="tp", bufs=2))
        ctx.enter_context(tc.manual_schedule())

        ident = const.tile([P, P], F32)
        make_identity(nc, ident[:])

        v_sb = const.tile([P, KV_HEADS, TOKEN_TILES, HEAD_DIM], BF16)

        def load_g(j, chunk):
            g_raw = raw_g.tile([P, CHUNK], BF16, tag="g_raw")
            nc.sync.dma_start(out=g_raw[:], in_=g_view[:, j, chunk * CHUNK : (chunk + 1) * CHUNK])
            return g_raw

        first_g = load_g(0, 0)

        sc_rows = const.tile([P, K_PASS], BF16)
        nc.vector.memset(sc_rows[:], 0.0)
        nc.sync.dma_start(
            out=sc_rows[0:PASSES, :], in_=attn_scale.rearrange("(r w) -> r w", w=K_PASS)
        )
        table = const.tile([P, 2], F32)
        nc.vector.memset(table[:, 0:1], 0.0)
        nc.scalar.copy(out=table[:, 1:2], in_=table[:, 0:1])
        sc_ps = tp_pool.tile([P, PACK, P], F32, tag="tp")
        for u in range(2):
            nc.tensor.transpose(sc_ps[:, u, :], sc_rows[:].bitcast(F32)[:, u::2], ident[:])
        sc_t = const.tile([P, PASSES * PACK], BF16)
        nc.vector.tensor_copy(
            out=sc_t[:].bitcast(F32).rearrange("p (c u) -> p c u", u=2),
            in_=sc_ps[:, 0:2, 0:PASSES].rearrange("p u c -> p c u"),
        )

        gs_codes = keep.tile([P, TOKEN_TILES * PASSES * P], U32, align_bytes=64)
        gs_scales = keep.tile([P, TOKEN_TILES * PASSES * P], U8, align_bytes=64)
        w_codes = keep.tile([P, PASSES * C], U32, align_bytes=64)
        w_scales = keep.tile([P, PASSES * C], U8, align_bytes=64)

        sq = const.tile([P, KV_HEADS, TOKEN_TILES, HEAD_DIM], BF16)
        ss = [const.tile([P, 2 * TOKEN_TILES], F32, name="ss%d" % n) for n in range(HALVES)]

        acc = {}
        for n in range(HALVES):
            for j in range(EARLY_TILES):
                acc[(j, n)] = acc_pool.tile([P, N_TILE], F32, name="acc%d%d" % (j, n))

        def load_w(c):
            w_raw = raw.tile([P, PACK, C], BF16, tag="w_raw")
            nc.sync.dma_start(
                out=w_raw[:],
                in_=wo[c * K_PASS : (c + 1) * K_PASS, :].rearrange("(q t) n -> q t n", t=PACK),
            )
            return w_raw

        def transpose_and_scale_g(g_raw, gs_t, chunk, b):
            words = g_raw[:].bitcast(F32)
            xt = tp_pool.tile([P, PACK, P], F32, tag="tp")
            for c in range(2):
                for u in range(2):
                    w0 = (2 * b + c) * 2 * P
                    nc.tensor.transpose(
                        xt[:, 2 * c : 2 * c + 2, :].rearrange("p u r -> p (u r)")[:, u::2],
                        words[:, w0 + u : w0 + 2 * P : 2],
                        ident[:],
                    )
            first = (chunk * CHUNK_PASSES + 2 * b) * PACK
            nc.vector.tensor_tensor(
                out=gs_t[:, b * 2 * K_PASS : (b + 1) * 2 * K_PASS].rearrange(
                    "p (c r u e) -> p c r u e", c=2, u=2, e=2
                ),
                in0=xt[:]
                .rearrange("p s r -> p (s r)")
                .bitcast(BF16)
                .rearrange("p (c r u e) -> p c r u e", u=2, c=2, e=2),
                in1=sc_t[:, first : first + 2 * PACK]
                .rearrange("p (c u e) -> p c u e", c=2, u=2)
                .unsqueeze(2)
                .to_broadcast([P, 2, P, 2, 2]),
                op=ALU.mult,
            )

        def quantise_g(gs_t, j, chunk):
            col = (j * PASSES + chunk * CHUNK_PASSES) * P
            cols = slice(col, col + CHUNK_PASSES * P)
            nc.vector.quantize_mx(
                out=gs_codes[:, cols].bitcast(E5M2_X4),
                scales=gs_scales[:, cols],
                in_=gs_t[:],
            )

        def regroup_w(w_halves, scalar_cols):
            w_grp = stage.tile([P, C, PACK], BF16, tag="w_grp", align_bytes=64)
            for copy, cols in (
                (nc.scalar.copy, slice(0, N_TILE)),
                (nc.scalar.copy, slice(N_TILE, scalar_cols)),
                (nc.vector.tensor_copy, slice(scalar_cols, C)),
            ):
                if cols.start >= cols.stop:
                    continue
                n = cols.start // N_TILE
                copy(
                    out=w_grp[:, cols, :].rearrange("p (c i) t -> p c t i", i=4),
                    in_=w_halves[n][:, :, cols.start - n * N_TILE : cols.stop - n * N_TILE].rearrange(
                        "p t (c i) -> p c t i", i=4
                    ),
                )
            return w_grp

        def quantise_w(w_grp, c, pieces):
            width = C // pieces
            for i in range(pieces):
                cols = slice(c * C + i * width, c * C + (i + 1) * width)
                nc.vector.quantize_mx(
                    out=w_codes[:, cols].bitcast(E4M3_X4),
                    scales=w_scales[:, cols],
                    in_=w_grp[:, i * width : (i + 1) * width, :].rearrange("p n t -> p (n t)"),
                )

        def multiply(j, c, n):
            g_cols = slice((j * PASSES + c) * P, (j * PASSES + c + 1) * P)
            w_cols = slice(c * C + n * N_TILE, c * C + (n + 1) * N_TILE)
            nc.tensor.matmul_mx(
                out=acc[(j, n)][:],
                lhsT=gs_codes[:, g_cols].bitcast(E5M2_X4),
                lhsT_scale=gs_scales[:, g_cols],
                rhs=w_codes[:, w_cols].bitcast(E4M3_X4),
                rhs_scale=w_scales[:, w_cols],
                start=(c == 0),
                stop=(c == PASSES - 1),
            )

        def square_v(h):
            for j in range(TOKEN_TILES):
                nc.scalar.activation(
                    out=sq[:, h, j, :],
                    in_=v_sb[:, h, j, :],
                    func=ACT.Square,
                    accum_out=ss[h // 2][:, (h % 2) * TOKEN_TILES + j : (h % 2) * TOKEN_TILES + j + 1],
                )

        late_passes = [(c, n) for n in range(HALVES) for c in range(PASSES)]

        def multiply_early(c, n):
            for early in range(EARLY_TILES):
                multiply(early, c, n)

        def multiply_late(count):
            for c, n in late_passes[:count]:
                multiply(EARLY_TILES, c, n)
            late_passes[:count] = []

        g_raw_of, w_raw_of, w_grp_of = {}, {}, {}
        chunks_in = {}
        for slot in range(PASSES):
            start = sum(CHUNKS_OF[:slot])
            chunks_in[slot] = list(range(start, start + CHUNKS_OF[slot]))
        last_chunk_slot = max(s for s in chunks_in if chunks_in[s])
        for slot in range(-LOAD_AHEAD, PASSES + 1):
            ahead = slot + LOAD_AHEAD
            preparing = 0 <= slot < PASSES
            if ahead < PASSES:
                for i in chunks_in[ahead]:
                    if i == 0:
                        g_raw_of[i] = first_g
                    else:
                        g_raw_of[i] = load_g(i % TOKEN_TILES, i // TOKEN_TILES)
                w_raw = load_w(ahead)
                w_raw_of[ahead] = [w_raw[:, :, n * N_TILE : (n + 1) * N_TILE] for n in range(HALVES)]
            if ahead == PASSES - 1:
                nc.sync.dma_start(out=v_sb[:].rearrange("p h j d -> p h (j d)"), in_=v_view)
            if slot < 0:
                continue
            chunks = chunks_in.get(slot, [])
            scaled = []

            def scale_next():
                if len(scaled) < len(chunks):
                    i = chunks[len(scaled)]
                    gs_t = stage.tile([P, CHUNK], BF16, tag="gs_t", align_bytes=64)
                    for b in range(2):
                        transpose_and_scale_g(g_raw_of[i], gs_t, i // TOKEN_TILES, b)
                    scaled.append((gs_t, i))

            passes = PASSES_IN[slot]
            scale_next()
            if slot == 0:
                while len(scaled) < len(chunks):
                    scale_next()
                for gs_t, i in scaled:
                    quantise_g(gs_t, i % TOKEN_TILES, i // TOKEN_TILES)
            if preparing:
                w_grp_of[slot] = regroup_w(w_raw_of[slot], SCALAR_COLS[len(chunks)])
            if slot == last_chunk_slot + 1:
                for n in range(HALVES):
                    acc[(EARLY_TILES, n)] = tp_pool.tile(
                        [P, N_TILE], F32, tag="tp", name="acc_late%d" % n
                    )
            if slot == PASSES - 1:
                for h in range(SQUARES_FIRST):
                    square_v(h)
            if slot == PASSES:
                quantise_w(w_grp_of[slot - 1], slot - 1, HALVES)
            elif slot > 0:
                quantise_w(w_grp_of[slot - 1], slot - 1, 1)
            multiply_late(LATE_BEFORE.get(slot, 0))
            for c in passes[:1]:
                multiply_early(c, 0)
            scale_next()
            for gs_t, i in scaled if slot > 0 else ():
                quantise_g(gs_t, i % TOKEN_TILES, i // TOKEN_TILES)
            for c in passes[:1]:
                multiply_early(c, 1)
            for c in passes[1:]:
                multiply_early(c, 0)
                multiply_early(c, 1)
            multiply_late(LATE_IN.get(slot, 0))
        multiply_late(len(late_passes))

        neg_ss = [const.tile([P, 2, TOKEN_TILES], F32, name="neg_ss%d" % n) for n in range(HALVES)]
        neg_inv = [const.tile([P, 2, TOKEN_TILES], F32, name="neg_inv%d" % n) for n in range(HALVES)]

        def negate_norms(n):
            nc.vector.tensor_scalar(
                out=neg_ss[n][:].rearrange("p h j -> p (h j)"),
                in0=ss[n][:],
                scalar1=1e-24,
                scalar2=-1.0,
                op0=ALU.max,
                op1=ALU.mult,
            )

        def invert_norms(n):
            nc.vector.reciprocal(out=neg_inv[n][:], in_=neg_ss[n][:])

        banks = [(j, n) for n in range(HALVES) for j in range(EARLY_TILES)]
        banks += [(EARLY_TILES, n) for n in range(HALVES)]

        def start_projection(j, n):
            prod = tail.tile([P, BANK_HEADS, HEAD_DIM], F32, tag="prod")
            nc.vector.tensor_tensor(
                out=prod[:].rearrange("p (h g) d -> p h g d", g=GROUP),
                in0=acc[(j, n)][:].rearrange("p (h g d) -> p h g d", g=GROUP, d=HEAD_DIM),
                in1=v_sb[:, 2 * n : 2 * n + 2, j, :]
                .unsqueeze(2)
                .to_broadcast([P, 2, GROUP, HEAD_DIM]),
                op=ALU.mult,
            )
            if (j, n) == banks[0]:
                invert_norms(n)
            coef = tail.tile([P, BANK_HEADS], F32, tag="coef")
            for q in range(BANK_HEADS):
                nc.scalar.activation(
                    out=prod[:, q, :],
                    in_=prod[:, q, :],
                    func=ACT.Copy,
                    scale=neg_inv[n][:, q // GROUP, j : j + 1],
                    accum_out=coef[:, q : q + 1],
                )
            return coef

        def finish_projection(j, n, coef, pieces=1):
            res = tail.tile([P, BANK_HEADS, HEAD_DIM], F32, tag="res")
            for q in range(BANK_HEADS):
                nc.vector.scalar_tensor_tensor(
                    out=res[:, q, :],
                    in0=v_sb[:, 2 * n + q // GROUP, j, :],
                    scalar=coef[:, q : q + 1],
                    in1=acc[(j, n)][:, q * HEAD_DIM : (q + 1) * HEAD_DIM],
                    op0=ALU.mult,
                    op1=ALU.add,
                )
                width = BANK_HEADS // pieces
                if (q + 1) % width == 0:
                    q0 = q + 1 - width
                    nc.sync.dma_start(
                        out=out_view[:, j, n * BANK_HEADS + q0 : n * BANK_HEADS + q + 1, :],
                        in_=res[:, q0 : q + 1, :],
                    )

        coefs = {}
        negate_norms(0)
        for b, bank in enumerate(banks):
            coefs[bank] = start_projection(*bank)
            if b < KV_HEADS - SQUARES_FIRST:
                square_v(SQUARES_FIRST + b)
            if b == EARLY_TILES - 1:
                negate_norms(1)
            if b >= FINISH_LAG:
                finish_projection(*banks[b - FINISH_LAG], coefs[banks[b - FINISH_LAG]])
            if b == EARLY_TILES - 1:
                invert_norms(1)
        for bank in banks[-FINISH_LAG:]:
            finish_projection(*bank, coefs[bank], pieces=2)
